import numpy as np
import ml_dtypes


def mxq(x, axis, fmt="e4m3"):
    dtype, down = {"e4m3": (ml_dtypes.float8_e4m3fn, 7), "e5m2": (ml_dtypes.float8_e5m2, 14)}[fmt]
    v = np.moveaxis(np.asarray(x, np.float32).astype(ml_dtypes.bfloat16).astype(np.float64), axis, -1)
    blocks = v.reshape(v.shape[:-1] + (-1, 32))
    amax = np.abs(blocks).max(-1, keepdims=True)
    byte = np.maximum(np.where(amax > 0, np.frexp(amax)[1] - 1 + 127, 0) - down, 1)
    scale = np.exp2(byte - 127.0)
    codes = (blocks / scale).astype(np.float32).astype(dtype).astype(np.float64)
    return np.moveaxis((codes * scale).reshape(v.shape), -1, axis)


WIDE = False


def mx_kscale(k):
    if not WIDE:
        return np.ones(k)
    levels = np.array([30, -30])
    if k % 512:
        return np.exp2(np.random.permutation(np.resize(levels, k // 32))).repeat(32)
    a = np.empty((k // 512, 16))
    for p in range(k // 512):
        a[p, :8] = np.random.permutation(np.resize(levels, 8))
        for g in range(8):
            far = levels[np.abs(levels - a[p, g]) >= 10]
            a[p, g + 8] = far[np.random.randint(len(far))]
    return np.exp2(a.ravel()).repeat(32)


BF16 = ml_dtypes.bfloat16


def bf(x):
    return np.asarray(x, np.float32).astype(BF16)


def f64(x):
    return np.asarray(x).astype(np.float64)


B, N, W, H, A = 4, 256, 2048, 16, 128
HD = H * A


def make_sin_cos():
    lin = np.linspace(0.0, 1.0, A // 2)
    freqs = 10000.0 ** (-np.repeat(lin, 2))
    theta = np.arange(N, dtype=np.float64)[:, None] * freqs[None, :]
    return np.sin(theta), np.cos(theta)


def apply_rope(y, sin, cos):
    yp = y.reshape(y.shape[:-1] + (A // 2, 2))
    yr = np.stack([-yp[..., 1], yp[..., 0]], axis=-1).reshape(y.shape)
    return y * cos + yr * sin


def setup_inputs():
    s = mx_kscale(W)
    return {"x": bf(np.random.standard_normal((B, N, W)) * s),
            "w": bf(np.random.standard_normal((HD, W)) / np.sqrt(W) / s[None, :])}


def reference(x, w):
    y = mxq(f64(x), 2, "e5m2") @ mxq(f64(w), 1, "e4m3").T
    y = y.reshape(B, N, H, A).transpose(0, 2, 1, 3)
    sin, cos = make_sin_cos()
    return apply_rope(y, sin, cos)

@@ -1,0 +1,222 @@
+import math
+from contextlib import ExitStack
+
+import concourse.mybir as mybir
+from concourse.masks import make_identity
+
+F32 = mybir.dt.float32
+BF16 = mybir.dt.bfloat16
+U32 = mybir.dt.uint32
+U8 = mybir.dt.uint8
+I32 = mybir.dt.int32
+E5X4 = mybir.dt.float8_e5m2_x4
+E4X4 = mybir.dt.float8_e4m3fn_x4
+ALU = mybir.AluOpType
+ACT = mybir.ActivationFunctionType
+
+B, N, W, H, A = 4, 256, 2048, 16, 128
+P = 128
+PASSES = W // 512
+FLOPS = 2 * B * N * W * H * A
+
+
+def tile_mha_pa_kernel(tc, x, w, out):
+    nc = tc.nc
+    with ExitStack() as ctx:
+        ctx.enter_context(tc.manual_schedule())
+        keep = ctx.enter_context(tc.tile_pool(name="keep", bufs=1))
+        stage = ctx.enter_context(tc.tile_pool(name="stage", bufs=3))
+        psum_t = ctx.enter_context(tc.psum_pool(name="psum_t", bufs=4))
+        psum_a = ctx.enter_context(tc.psum_pool(name="psum_a", bufs=4))
+
+        x_v = x.rearrange("b (p i) k -> b i p k", i=2)
+        w_v = w.rearrange("(h p) k -> h p k", p=P)
+        w_v2 = w.rearrange("(q e p) k -> q p e k", p=P, e=2)
+        o_v = out.rearrange("b h (p i) a -> b p h i a", i=2)
+        w0_raw = {}
+        for gp in range(2):
+            for hh in range(4):
+                w0_raw[(hh, gp)] = keep.tile([P, 1024], BF16, name="w0raw%d_%d" % (hh, gp))
+                nc.sync.dma_start(out=w0_raw[(hh, gp)][:], in_=w_v[hh][:, 1024 * gp:1024 * (gp + 1)])
+        x_raw = []
+        for m in range(2 * B):
+            x_raw.append(keep.tile([P, W], BF16, name="xraw%d" % m))
+            nc.sync.dma_start(out=x_raw[m][:], in_=x_v[m // 2][m % 2])
+        w_raw = {}
+        for q in range(2, 8):
+            w_raw[q] = keep.tile([P, 2, W], BF16, name="wraw%d" % q)
+            nc.sync.dma_start(out=w_raw[q][:], in_=w_v2[q])
+
+        warm = keep.tile([P, 1], F32, name="warm")
+        nc.vector.memset(warm[:], 0.0)
+        nc.scalar.activation(out=warm[:], in_=warm[:], func=ACT.Sin)
+
+        ident = keep.tile([P, P], F32, name="ident")
+        make_identity(nc, ident[:])
+
+        pos = keep.tile([P, 2], F32, name="pos")
+        nc.gpsimd.iota(pos[:], pattern=[[1, 2]], base=0, channel_multiplier=2,
+                       allow_small_or_imprecise_dtypes=True)
+        ones = keep.tile([P, 8], F32, name="ones")
+        nc.vector.memset(ones[:], 1.0)
+        frq = keep.tile([P, 8, 8], F32, name="frq")
+        for a in range(8):
+            nc.vector.tensor_scalar(out=frq[:, a, :], in0=ones[:], scalar1=10000.0 ** (-8.0 * a / 63.0),
+                                    scalar2=None, op0=ALU.mult)
+        for c in range(1, 8):
+            nc.vector.tensor_scalar(out=frq[:, :, c], in0=frq[:, :, c], scalar1=10000.0 ** (-1.0 * c / 63.0),
+                                    scalar2=None, op0=ALU.mult)
+        ang = keep.tile([P, 2, 2, 64], F32, name="ang")
+        for i in range(2):
+            for s in range(2):
+                nc.vector.tensor_scalar(out=ang[:, i, s, :], in0=frq[:].rearrange("p a c -> p (a c)"),
+                                        scalar1=pos[:, i:i + 1], scalar2=s * math.pi / 2.0,
+                                        op0=ALU.mult, op1=ALU.add)
+        ang_f = ang[:].rearrange("p i s f -> p (i s f)")
+        turns_i = keep.tile([P, 256], I32, name="turns_i")
+        nc.vector.tensor_scalar(out=turns_i[:], in0=ang_f, scalar1=1.0 / (2.0 * math.pi), scalar2=None,
+                                op0=ALU.mult)
+        turns = keep.tile([P, 256], F32, name="turns")
+        nc.vector.tensor_copy(out=turns[:], in_=turns_i[:])
+        c_hi = 6.28125
+        c_lo = 2.0 * math.pi - c_hi
+        red1 = keep.tile([P, 256], F32, name="red1")
+        nc.vector.scalar_tensor_tensor(out=red1[:], in0=turns[:], scalar=-c_hi, in1=ang_f,
+                                       op0=ALU.mult, op1=ALU.add)
+        red2 = keep.tile([P, 256], F32, name="red2")
+        nc.vector.scalar_tensor_tensor(out=red2[:], in0=turns[:], scalar=-c_lo, in1=red1[:],
+                                       op0=ALU.mult, op1=ALU.add)
+        fold = keep.tile([P, 256], F32, name="fold")
+        nc.vector.tensor_scalar(out=fold[:], in0=red2[:], scalar1=math.pi, scalar2=-2.0 * math.pi,
+                                op0=ALU.is_gt, op1=ALU.mult)
+        red3 = keep.tile([P, 256], F32, name="red3")
+        nc.vector.tensor_tensor(out=red3[:], in0=red2[:], in1=fold[:], op=ALU.add)
+        fold2 = keep.tile([P, 256], F32, name="fold2")
+        nc.vector.tensor_scalar(out=fold2[:], in0=red3[:], scalar1=-math.pi, scalar2=2.0 * math.pi,
+                                op0=ALU.is_lt, op1=ALU.mult)
+        red4 = keep.tile([P, 256], F32, name="red4")
+        nc.vector.tensor_tensor(out=red4[:], in0=red3[:], in1=fold2[:], op=ALU.add)
+        sc = keep.tile([P, 2, 2, 64], F32, name="sc")
+        cos1 = keep.tile([P, 2, 64, 2], F32, name="cos1")
+        sin1 = keep.tile([P, 2, 64, 2], F32, name="sin1")
+        cos_t = keep.tile([P, 2, 4, A], F32, name="cos_t")
+        sin_t = keep.tile([P, 2, 4, A], F32, name="sin_t")
+
+        def finish_tables():
+            nc.scalar.activation(out=sc[:].rearrange("p i s f -> p (i s f)"), in_=red4[:], func=ACT.Sin)
+            nc.vector.tensor_copy(out=cos1[:, :, :, 0], in_=sc[:, :, 1, :])
+            nc.vector.tensor_copy(out=cos1[:, :, :, 1], in_=sc[:, :, 1, :])
+            nc.vector.tensor_scalar(out=sin1[:, :, :, 0], in0=sc[:, :, 0, :], scalar1=-1.0, scalar2=None,
+                                    op0=ALU.mult)
+            nc.vector.tensor_copy(out=sin1[:, :, :, 1], in_=sc[:, :, 0, :])
+            for hh in range(4):
+                nc.vector.tensor_copy(out=cos_t[:, :, hh, :], in_=cos1[:].rearrange("p i f e -> p i (f e)"))
+                nc.vector.tensor_copy(out=sin_t[:, :, hh, :], in_=sin1[:].rearrange("p i f e -> p i (f e)"))
+
+        x_codes = []
+        x_scales = []
+        for m in range(2 * B):
+            x_codes.append(keep.tile([P, PASSES * P], U32, name="xc%d" % m, align_bytes=64))
+            x_scales.append(keep.tile([P, PASSES * P], U8, name="xs%d" % m, align_bytes=64))
+        w_group = {}
+        w_codes = {}
+        w_scales = {}
+
+        def turn(words, dst):
+            tp = psum_t.tile([P, 2, 2, P], F32, name="tp")
+            for gg in range(2):
+                for u in range(2):
+                    nc.tensor.transpose(out=tp[:, gg, u, :], in_=words[:, 256 * gg + u:256 * (gg + 1):2],
+                                        identity=ident[:])
+            nc.scalar.copy(out=dst, in_=tp[:].rearrange("p a u r -> p a r u"))
+
+        def prep_w(c, gp):
+            if gp == 0:
+                w_group[c] = stage.tile([P, PASSES, 2048], BF16, name="gw", bufs=2, align_bytes=64)
+                w_codes[c] = stage.tile([P, PASSES, 512], U32, name="wc", bufs=2, align_bytes=64)
+                w_scales[c] = stage.tile([P, PASSES, 512], U8, name="ws", bufs=2, align_bytes=64)
+            gwords = w_group[c][:].bitcast(F32)
+            for hh in range(4):
+                if c == 0:
+                    words = w0_raw[(hh, gp)][:].bitcast(F32)
+                else:
+                    words = w_raw[2 * c + hh // 2][:, hh % 2, 1024 * gp:1024 * (gp + 1)].bitcast(F32)
+                turn(words, gwords[:, 2 * gp:2 * gp + 2, 256 * hh:256 * (hh + 1)].rearrange(
+                    "p a (r u) -> p a r u", u=2))
+            two = slice(2 * gp, 2 * gp + 2)
+            nc.vector.quantize_mx(out=w_codes[c][:, two, :].rearrange("p a n -> p (a n)").bitcast(E4X4),
+                                  scales=w_scales[c][:, two, :].rearrange("p a n -> p (a n)"),
+                                  in_=w_group[c][:, two, :].rearrange("p a n -> p (a n)"))
+
+        def prep_x(m):
+            gx = stage.tile([P, PASSES, 512], BF16, name="gx", align_bytes=64)
+            gwords = gx[:].bitcast(F32)
+            words = x_raw[m][:].bitcast(F32)
+            for gp in range(2):
+                turn(words[:, 512 * gp:512 * (gp + 1)],
+                     gwords[:, 2 * gp:2 * gp + 2, :].rearrange("p a (r u) -> p a r u", u=2))
+            nc.vector.quantize_mx(out=x_codes[m][:].bitcast(E5X4), scales=x_scales[m][:],
+                                  in_=gx[:].rearrange("p a n -> p (a n)"))
+
+        def product(m, c):
+            acc = psum_a.tile([P, 512], F32, name="acc")
+            for g in range(PASSES):
+                cols = slice(P * g, P * (g + 1))
+                nc.tensor.matmul_mx(out=acc[:], lhsT=x_codes[m][:, cols].bitcast(E5X4),
+                                    lhsT_scale=x_scales[m][:, cols],
+                                    rhs=w_codes[c][:, g, :].bitcast(E4X4), rhs_scale=w_scales[c][:, g, :],
+                                    start=(g == 0), stop=(g == PASSES - 1))
+            return acc
+
+        def rotate(acc, i, res, adder):
+            ta = stage.tile([P, 512], F32, name="ta")
+            tb = stage.tile([P, 512], F32, name="tb")
+            nc.vector.tensor_tensor(out=ta[:], in0=acc[:], in1=cos_t[:, i, :, :].rearrange("p h a -> p (h a)"),
+                                    op=ALU.mult)
+            nc.vector.tensor_tensor(out=tb[:].rearrange("p (f e) -> p f e", e=2),
+                                    in0=acc[:].rearrange("p (f e) -> p f e", e=2)[:, :, ::-1],
+                                    in1=sin_t[:, i, :, :].rearrange("p h (f e) -> p (h f) e", e=2),
+                                    op=ALU.mult)
+            adder.tensor_tensor(out=res[:, :, i, :], in0=ta[:].rearrange("p (h a) -> p h a", h=4),
+                                in1=tb[:].rearrange("p (h a) -> p h a", h=4), op=ALU.add)
+
+        results = {}
+
+        def head_tile(m, c):
+            b, i = m // 2, m % 2
+            last = (c == 3 and b == B - 1)
+            if i == 0:
+                results[b] = stage.tile([P, 4, 2, A], F32, name="res")
+            acc = product(m, c)
+            rotate(acc, i, results[b], nc.vector if (last and i == 1) else nc.gpsimd)
+            if last:
+                nc.sync.dma_start(out=o_v[b][:, 4 * c:4 * c + 4, i, :], in_=results[b][:, :, i, :])
+            elif i == 1:
+                nc.sync.dma_start(out=o_v[b][:, 4 * c:4 * c + 4, :, :], in_=results[b][:])
+
+        prep_w(0, 0)
+        finish_tables()
+        prep_w(0, 1)
+        for m in range(4):
+            prep_x(m)
+        head_tile(0, 0)
+        head_tile(1, 0)
+        prep_x(4)
+        prep_x(5)
+        head_tile(2, 0)
+        head_tile(3, 0)
+        prep_x(6)
+        prep_x(7)
+        head_tile(4, 0)
+        prep_w(1, 0)
+        head_tile(5, 0)
+        prep_w(1, 1)
+        head_tile(6, 0)
+        head_tile(7, 0)
+        for c in range(1, 4):
+            for m in range(8):
+                head_tile(m, c)
+                if c < 3 and m == 2:
+                    prep_w(c + 1, 0)
+                if c < 3 and m == 5:
+                    prep_w(c + 1, 1)

@@ -47,6 +47,9 @@ def tile_mha_pa_kernel(tc, x, w, out):
             w_raw[q] = keep.tile([P, 2, W], BF16, name="wraw%d" % q)
             nc.sync.dma_start(out=w_raw[q][:], in_=w_v2[q])
 
+        zeros = keep.tile([P, 512], BF16, name="zeros")
+        nc.vector.memset(zeros[:], 0.0)
+
         warm = keep.tile([P, 1], F32, name="warm")
         nc.vector.memset(warm[:], 0.0)
         nc.scalar.activation(out=warm[:], in_=warm[:], func=ACT.Sin)
@@ -80,22 +83,16 @@ def tile_mha_pa_kernel(tc, x, w, out):
         nc.vector.tensor_copy(out=turns[:], in_=turns_i[:])
         c_hi = 6.28125
         c_lo = 2.0 * math.pi - c_hi
-        red1 = keep.tile([P, 256], F32, name="red1")
-        nc.vector.scalar_tensor_tensor(out=red1[:], in0=turns[:], scalar=-c_hi, in1=ang_f,
+        nc.vector.scalar_tensor_tensor(out=ang_f, in0=turns[:], scalar=-c_hi, in1=ang_f,
                                        op0=ALU.mult, op1=ALU.add)
-        red2 = keep.tile([P, 256], F32, name="red2")
-        nc.vector.scalar_tensor_tensor(out=red2[:], in0=turns[:], scalar=-c_lo, in1=red1[:],
+        nc.vector.scalar_tensor_tensor(out=ang_f, in0=turns[:], scalar=-c_lo, in1=ang_f,
                                        op0=ALU.mult, op1=ALU.add)
-        fold = keep.tile([P, 256], F32, name="fold")
-        nc.vector.tensor_scalar(out=fold[:], in0=red2[:], scalar1=math.pi, scalar2=-2.0 * math.pi,
+        nc.vector.tensor_scalar(out=turns[:], in0=ang_f, scalar1=math.pi, scalar2=-2.0 * math.pi,
                                 op0=ALU.is_gt, op1=ALU.mult)
-        red3 = keep.tile([P, 256], F32, name="red3")
-        nc.vector.tensor_tensor(out=red3[:], in0=red2[:], in1=fold[:], op=ALU.add)
-        fold2 = keep.tile([P, 256], F32, name="fold2")
-        nc.vector.tensor_scalar(out=fold2[:], in0=red3[:], scalar1=-math.pi, scalar2=2.0 * math.pi,
+        nc.vector.tensor_tensor(out=ang_f, in0=ang_f, in1=turns[:], op=ALU.add)
+        nc.vector.tensor_scalar(out=turns[:], in0=ang_f, scalar1=-math.pi, scalar2=2.0 * math.pi,
                                 op0=ALU.is_lt, op1=ALU.mult)
-        red4 = keep.tile([P, 256], F32, name="red4")
-        nc.vector.tensor_tensor(out=red4[:], in0=red3[:], in1=fold2[:], op=ALU.add)
+        nc.vector.tensor_tensor(out=ang_f, in0=ang_f, in1=turns[:], op=ALU.add)
         sc = keep.tile([P, 2, 2, 64], F32, name="sc")
         cos1 = keep.tile([P, 2, 64, 2], F32, name="cos1")
         sin1 = keep.tile([P, 2, 64, 2], F32, name="sin1")
@@ -103,7 +100,7 @@ def tile_mha_pa_kernel(tc, x, w, out):
         sin_t = keep.tile([P, 2, 4, A], F32, name="sin_t")
 
         def finish_tables():
-            nc.scalar.activation(out=sc[:].rearrange("p i s f -> p (i s f)"), in_=red4[:], func=ACT.Sin)
+            nc.scalar.activation(out=sc[:].rearrange("p i s f -> p (i s f)"), in_=ang_f, func=ACT.Sin)
             nc.vector.tensor_copy(out=cos1[:, :, :, 0], in_=sc[:, :, 1, :])
             nc.vector.tensor_copy(out=cos1[:, :, :, 1], in_=sc[:, :, 1, :])
             nc.vector.tensor_scalar(out=sin1[:, :, :, 0], in0=sc[:, :, 0, :], scalar1=-1.0, scalar2=None,
@@ -118,17 +115,31 @@ def tile_mha_pa_kernel(tc, x, w, out):
         for m in range(2 * B):
             x_codes.append(keep.tile([P, PASSES * P], U32, name="xc%d" % m, align_bytes=64))
             x_scales.append(keep.tile([P, PASSES * P], U8, name="xs%d" % m, align_bytes=64))
+        w_sorted = {}
         w_group = {}
         w_codes = {}
         w_scales = {}
 
-        def turn(words, dst):
+        def spin(count):
+            idle = psum_a.tile([P, 512], F32, name="acc")
+            for r in range(count):
+                nc.tensor.matmul(out=idle[:], lhsT=zeros[:, 0:P], rhs=zeros[:], start=True, stop=True)
+
+        def turn(srcs, dst):
             tp = psum_t.tile([P, 2, 2, P], F32, name="tp")
-            for gg in range(2):
-                for u in range(2):
-                    nc.tensor.transpose(out=tp[:, gg, u, :], in_=words[:, 256 * gg + u:256 * (gg + 1):2],
-                                        identity=ident[:])
+            for j in range(4):
+                nc.tensor.transpose(out=tp[:, j // 2, j % 2, :], in_=srcs[j], identity=ident[:])
             nc.scalar.copy(out=dst, in_=tp[:].rearrange("p a u r -> p a r u"))
+
+        def every_second(words):
+            return [words[:, 256 * gg + u:256 * (gg + 1):2] for gg in range(2) for u in range(2)]
+
+        def sort_w(c, gp):
+            w_sorted[(c, gp)] = stage.tile([P, 4, 4, P], F32, name="wsort", bufs=2)
+            for hh in range(4):
+                words = w_raw[2 * c + hh // 2][:, hh % 2, 1024 * gp:1024 * (gp + 1)].bitcast(F32)
+                nc.scalar.copy(out=w_sorted[(c, gp)][:, hh, :, :].rearrange("p (a u) j -> p a u j", u=2),
+                               in_=words.rearrange("p (a j u) -> p a u j", a=2, u=2))
 
         def prep_w(c, gp):
             if gp == 0:
@@ -138,10 +149,10 @@ def tile_mha_pa_kernel(tc, x, w, out):
             gwords = w_group[c][:].bitcast(F32)
             for hh in range(4):
                 if c == 0:
-                    words = w0_raw[(hh, gp)][:].bitcast(F32)
+                    srcs = every_second(w0_raw[(hh, gp)][:].bitcast(F32))
                 else:
-                    words = w_raw[2 * c + hh // 2][:, hh % 2, 1024 * gp:1024 * (gp + 1)].bitcast(F32)
-                turn(words, gwords[:, 2 * gp:2 * gp + 2, 256 * hh:256 * (hh + 1)].rearrange(
+                    srcs = [w_sorted[(c, gp)][:, hh, j, :] for j in range(4)]
+                turn(srcs, gwords[:, 2 * gp:2 * gp + 2, 256 * hh:256 * (hh + 1)].rearrange(
                     "p a (r u) -> p a r u", u=2))
             two = slice(2 * gp, 2 * gp + 2)
             nc.vector.quantize_mx(out=w_codes[c][:, two, :].rearrange("p a n -> p (a n)").bitcast(E4X4),
@@ -149,11 +160,11 @@ def tile_mha_pa_kernel(tc, x, w, out):
                                   in_=w_group[c][:, two, :].rearrange("p a n -> p (a n)"))
 
         def prep_x(m):
-            gx = stage.tile([P, PASSES, 512], BF16, name="gx", align_bytes=64)
+            gx = stage.tile([P, PASSES, 512], BF16, name="gx", bufs=2, align_bytes=64)
             gwords = gx[:].bitcast(F32)
             words = x_raw[m][:].bitcast(F32)
             for gp in range(2):
-                turn(words[:, 512 * gp:512 * (gp + 1)],
+                turn(every_second(words[:, 512 * gp:512 * (gp + 1)]),
                      gwords[:, 2 * gp:2 * gp + 2, :].rearrange("p a (r u) -> p a r u", u=2))
             nc.vector.quantize_mx(out=x_codes[m][:].bitcast(E5X4), scales=x_scales[m][:],
                                   in_=gx[:].rearrange("p a n -> p (a n)"))
@@ -194,19 +205,27 @@ def tile_mha_pa_kernel(tc, x, w, out):
             elif i == 1:
                 nc.sync.dma_start(out=o_v[b][:, 4 * c:4 * c + 4, :, :], in_=results[b][:])
 
+        spin(6)
         prep_w(0, 0)
+        spin(2)
         finish_tables()
         prep_w(0, 1)
-        for m in range(4):
-            prep_x(m)
+        spin(2)
+        prep_x(0)
+        prep_x(1)
+        spin(2)
+        prep_x(2)
+        prep_x(3)
         head_tile(0, 0)
         head_tile(1, 0)
         prep_x(4)
         prep_x(5)
         head_tile(2, 0)
         head_tile(3, 0)
+        sort_w(1, 0)
         prep_x(6)
         prep_x(7)
+        sort_w(1, 1)
         head_tile(4, 0)
         prep_w(1, 0)
         head_tile(5, 0)
@@ -216,7 +235,11 @@ def tile_mha_pa_kernel(tc, x, w, out):
         for c in range(1, 4):
             for m in range(8):
                 head_tile(m, c)
+                if c < 3 and m == 0:
+                    sort_w(c + 1, 0)
                 if c < 3 and m == 2:
                     prep_w(c + 1, 0)
+                if c < 3 and m == 3:
+                    sort_w(c + 1, 1)
                 if c < 3 and m == 5:
                     prep_w(c + 1, 1)

@@ -19,6 +19,9 @@ P = 128
 PASSES = W // 512
 FLOPS = 2 * B * N * W * H * A
 
+V_ADDS = (1, 4)
+V_ADDS_LAST = (1, 3, 5, 7)
+
 
 def tile_mha_pa_kernel(tc, x, w, out):
     nc = tc.nc
@@ -43,12 +46,13 @@ def tile_mha_pa_kernel(tc, x, w, out):
             x_raw.append(keep.tile([P, W], BF16, name="xraw%d" % m))
             nc.sync.dma_start(out=x_raw[m][:], in_=x_v[m // 2][m % 2])
         w_raw = {}
-        for q in range(2, 8):
-            w_raw[q] = keep.tile([P, 2, W], BF16, name="wraw%d" % q)
+
+        def load_w(q):
+            w_raw[q] = stage.tile([P, 2, W], BF16, name="wraw", bufs=4)
             nc.sync.dma_start(out=w_raw[q][:], in_=w_v2[q])
 
-        zeros = keep.tile([P, 512], BF16, name="zeros")
-        nc.vector.memset(zeros[:], 0.0)
+        for q in range(2, 6):
+            load_w(q)
 
         warm = keep.tile([P, 1], F32, name="warm")
         nc.vector.memset(warm[:], 0.0)
@@ -115,15 +119,12 @@ def tile_mha_pa_kernel(tc, x, w, out):
         for m in range(2 * B):
             x_codes.append(keep.tile([P, PASSES * P], U32, name="xc%d" % m, align_bytes=64))
             x_scales.append(keep.tile([P, PASSES * P], U8, name="xs%d" % m, align_bytes=64))
+        x_sorted = {}
+        x_group = {}
         w_sorted = {}
         w_group = {}
         w_codes = {}
         w_scales = {}
-
-        def spin(count):
-            idle = psum_a.tile([P, 512], F32, name="acc")
-            for r in range(count):
-                nc.tensor.matmul(out=idle[:], lhsT=zeros[:, 0:P], rhs=zeros[:], start=True, stop=True)
 
         def turn(srcs, dst):
             tp = psum_t.tile([P, 2, 2, P], F32, name="tp")
@@ -134,18 +135,25 @@ def tile_mha_pa_kernel(tc, x, w, out):
         def every_second(words):
             return [words[:, 256 * gg + u:256 * (gg + 1):2] for gg in range(2) for u in range(2)]
 
-        def sort_w(c, gp):
+        def sort_words(copy, dst, words):
+            copy(out=dst.rearrange("p (a u) j -> p a u j", u=2),
+                 in_=words.rearrange("p (a j u) -> p a u j", a=2, u=2))
+
+        def sort_w(c, gp, copy):
             w_sorted[(c, gp)] = stage.tile([P, 4, 4, P], F32, name="wsort", bufs=2)
             for hh in range(4):
-                words = w_raw[2 * c + hh // 2][:, hh % 2, 1024 * gp:1024 * (gp + 1)].bitcast(F32)
-                nc.scalar.copy(out=w_sorted[(c, gp)][:, hh, :, :].rearrange("p (a u) j -> p a u j", u=2),
-                               in_=words.rearrange("p (a j u) -> p a u j", a=2, u=2))
+                sort_words(copy, w_sorted[(c, gp)][:, hh, :, :],
+                           w_raw[2 * c + hh // 2][:, hh % 2, 1024 * gp:1024 * (gp + 1)].bitcast(F32))
 
-        def prep_w(c, gp):
+        def sort_x(m):
+            x_sorted[m] = stage.tile([P, 2, 4, P], F32, name="xsort", bufs=2)
+            for gp in range(2):
+                sort_words(nc.scalar.copy, x_sorted[m][:, gp, :, :],
+                           x_raw[m][:, 1024 * gp:1024 * (gp + 1)].bitcast(F32))
+
+        def turn_w(c, gp):
             if gp == 0:
                 w_group[c] = stage.tile([P, PASSES, 2048], BF16, name="gw", bufs=2, align_bytes=64)
-                w_codes[c] = stage.tile([P, PASSES, 512], U32, name="wc", bufs=2, align_bytes=64)
-                w_scales[c] = stage.tile([P, PASSES, 512], U8, name="ws", bufs=2, align_bytes=64)
             gwords = w_group[c][:].bitcast(F32)
             for hh in range(4):
                 if c == 0:
@@ -154,92 +162,135 @@ def tile_mha_pa_kernel(tc, x, w, out):
                     srcs = [w_sorted[(c, gp)][:, hh, j, :] for j in range(4)]
                 turn(srcs, gwords[:, 2 * gp:2 * gp + 2, 256 * hh:256 * (hh + 1)].rearrange(
                     "p a (r u) -> p a r u", u=2))
+
+        def quant_w(c, gp):
+            if gp == 0:
+                w_codes[c] = stage.tile([P, PASSES, 512], U32, name="wc", bufs=2, align_bytes=64)
+                w_scales[c] = stage.tile([P, PASSES, 512], U8, name="ws", bufs=2, align_bytes=64)
             two = slice(2 * gp, 2 * gp + 2)
             nc.vector.quantize_mx(out=w_codes[c][:, two, :].rearrange("p a n -> p (a n)").bitcast(E4X4),
                                   scales=w_scales[c][:, two, :].rearrange("p a n -> p (a n)"),
                                   in_=w_group[c][:, two, :].rearrange("p a n -> p (a n)"))
 
-        def prep_x(m):
-            gx = stage.tile([P, PASSES, 512], BF16, name="gx", bufs=2, align_bytes=64)
-            gwords = gx[:].bitcast(F32)
-            words = x_raw[m][:].bitcast(F32)
+        def turn_x(m):
+            x_group[m] = stage.tile([P, PASSES, 512], BF16, name="gx", bufs=2, align_bytes=64)
+            gwords = x_group[m][:].bitcast(F32)
             for gp in range(2):
-                turn(every_second(words[:, 512 * gp:512 * (gp + 1)]),
-                     gwords[:, 2 * gp:2 * gp + 2, :].rearrange("p a (r u) -> p a r u", u=2))
+                if m in x_sorted:
+                    srcs = [x_sorted[m][:, gp, j, :] for j in range(4)]
+                else:
+                    srcs = every_second(x_raw[m][:, 1024 * gp:1024 * (gp + 1)].bitcast(F32))
+                turn(srcs, gwords[:, 2 * gp:2 * gp + 2, :].rearrange("p a (r u) -> p a r u", u=2))
+
+        def quant_x(m):
             nc.vector.quantize_mx(out=x_codes[m][:].bitcast(E5X4), scales=x_scales[m][:],
-                                  in_=gx[:].rearrange("p a n -> p (a n)"))
+                                  in_=x_group[m][:].rearrange("p a n -> p (a n)"))
+
+        sums = {}
+        part_a = {}
+        part_b = {}
+        results = {}
+        added = set()
 
         def product(m, c):
-            acc = psum_a.tile([P, 512], F32, name="acc")
+            sums[(m, c)] = psum_a.tile([P, 512], F32, name="acc")
             for g in range(PASSES):
                 cols = slice(P * g, P * (g + 1))
-                nc.tensor.matmul_mx(out=acc[:], lhsT=x_codes[m][:, cols].bitcast(E5X4),
+                nc.tensor.matmul_mx(out=sums[(m, c)][:], lhsT=x_codes[m][:, cols].bitcast(E5X4),
                                     lhsT_scale=x_scales[m][:, cols],
                                     rhs=w_codes[c][:, g, :].bitcast(E4X4), rhs_scale=w_scales[c][:, g, :],
                                     start=(g == 0), stop=(g == PASSES - 1))
-            return acc
 
-        def rotate(acc, i, res, adder):
-            ta = stage.tile([P, 512], F32, name="ta")
-            tb = stage.tile([P, 512], F32, name="tb")
-            nc.vector.tensor_tensor(out=ta[:], in0=acc[:], in1=cos_t[:, i, :, :].rearrange("p h a -> p (h a)"),
+        def mul_a(m, c):
+            part_a[(m, c)] = stage.tile([P, 512], F32, name="ta")
+            nc.vector.tensor_tensor(out=part_a[(m, c)][:], in0=sums[(m, c)][:],
+                                    in1=cos_t[:, m % 2, :, :].rearrange("p h a -> p (h a)"), op=ALU.mult)
+
+        def mul_b(m, c):
+            part_b[(m, c)] = stage.tile([P, 512], F32, name="tb")
+            nc.vector.tensor_tensor(out=part_b[(m, c)][:].rearrange("p (f e) -> p f e", e=2),
+                                    in0=sums[(m, c)][:].rearrange("p (f e) -> p f e", e=2)[:, :, ::-1],
+                                    in1=sin_t[:, m % 2, :, :].rearrange("p h (f e) -> p (h f) e", e=2),
                                     op=ALU.mult)
-            nc.vector.tensor_tensor(out=tb[:].rearrange("p (f e) -> p f e", e=2),
-                                    in0=acc[:].rearrange("p (f e) -> p f e", e=2)[:, :, ::-1],
-                                    in1=sin_t[:, i, :, :].rearrange("p h (f e) -> p (h f) e", e=2),
-                                    op=ALU.mult)
-            adder.tensor_tensor(out=res[:, :, i, :], in0=ta[:].rearrange("p (h a) -> p h a", h=4),
-                                in1=tb[:].rearrange("p (h a) -> p h a", h=4), op=ALU.add)
 
-        results = {}
-
-        def head_tile(m, c):
+        def add(m, c, engine):
             b, i = m // 2, m % 2
-            last = (c == 3 and b == B - 1)
-            if i == 0:
-                results[b] = stage.tile([P, 4, 2, A], F32, name="res")
-            acc = product(m, c)
-            rotate(acc, i, results[b], nc.vector if (last and i == 1) else nc.gpsimd)
-            if last:
-                nc.sync.dma_start(out=o_v[b][:, 4 * c:4 * c + 4, i, :], in_=results[b][:, :, i, :])
-            elif i == 1:
-                nc.sync.dma_start(out=o_v[b][:, 4 * c:4 * c + 4, :, :], in_=results[b][:])
+            if (b, c) not in results:
+                results[(b, c)] = stage.tile([P, 4, 2, A], F32, name="res")
+            res = results[(b, c)]
+            engine.tensor_tensor(out=res[:, :, i, :], in0=part_a[(m, c)][:].rearrange("p (h a) -> p h a", h=4),
+                                 in1=part_b[(m, c)][:].rearrange("p (h a) -> p h a", h=4), op=ALU.add)
+            added.add((m, c))
+            if c == 3 and b == B - 1:
+                nc.sync.dma_start(out=o_v[b][:, 4 * c:4 * c + 4, i, :], in_=res[:, :, i, :])
+            elif (2 * b, c) in added and (2 * b + 1, c) in added:
+                nc.sync.dma_start(out=o_v[b][:, 4 * c:4 * c + 4, :, :], in_=res[:])
 
-        spin(6)
-        prep_w(0, 0)
-        spin(2)
+        late_adds = []
+        late_quants = []
+
+        def flush():
+            for (m, c) in late_adds:
+                add(m, c, nc.vector)
+            late_adds.clear()
+            for (kind, p0, p1) in late_quants:
+                if kind == "x":
+                    quant_x(p0)
+                else:
+                    quant_w(p0, p1)
+            late_quants.clear()
+
+        turn_w(0, 0)
+        quant_w(0, 0)
         finish_tables()
-        prep_w(0, 1)
-        spin(2)
-        prep_x(0)
-        prep_x(1)
-        spin(2)
-        prep_x(2)
-        prep_x(3)
-        head_tile(0, 0)
-        head_tile(1, 0)
-        prep_x(4)
-        prep_x(5)
-        head_tile(2, 0)
-        head_tile(3, 0)
-        sort_w(1, 0)
-        prep_x(6)
-        prep_x(7)
-        sort_w(1, 1)
-        head_tile(4, 0)
-        prep_w(1, 0)
-        head_tile(5, 0)
-        prep_w(1, 1)
-        head_tile(6, 0)
-        head_tile(7, 0)
-        for c in range(1, 4):
+        turn_w(0, 1)
+        quant_w(0, 1)
+        for m in range(4):
+            turn_x(m)
+            quant_x(m)
+        for c in range(4):
             for m in range(8):
-                head_tile(m, c)
-                if c < 3 and m == 0:
-                    sort_w(c + 1, 0)
-                if c < 3 and m == 2:
-                    prep_w(c + 1, 0)
-                if c < 3 and m == 3:
-                    sort_w(c + 1, 1)
-                if c < 3 and m == 5:
-                    prep_w(c + 1, 1)
+                product(m, c)
+                run = False
+                if c == 0 and m == 1:
+                    sort_x(4)
+                    sort_x(5)
+                    turn_x(4)
+                    turn_x(5)
+                    late_quants.extend([("x", 4, 0), ("x", 5, 0)])
+                    run = True
+                if c == 0 and m == 3:
+                    sort_w(1, 0, nc.vector.tensor_copy)
+                    sort_x(6)
+                    sort_x(7)
+                    turn_x(6)
+                    turn_x(7)
+                    late_quants.extend([("x", 6, 0), ("x", 7, 0)])
+                    sort_w(1, 1, nc.vector.tensor_copy)
+                    load_w(6)
+                    load_w(7)
+                    run = True
+                if c == 0 and m in (4, 5):
+                    turn_w(1, m - 4)
+                    late_quants.append(("w", 1, m - 4))
+                    run = True
+                if 0 < c < 3 and m == 2:
+                    sort_w(c + 1, 1, nc.scalar.copy)
+                if 0 < c < 3 and m in (1, 5):
+                    turn_w(c + 1, m // 4)
+                    late_quants.append(("w", c + 1, m // 4))
+                    run = True
+                if c < 2 and m == 6:
+                    sort_w(c + 2, 0, nc.scalar.copy)
+                if m in (V_ADDS_LAST if c == 3 else V_ADDS):
+                    mul_a(m, c)
+                    mul_b(m, c)
+                    late_adds.append((m, c))
+                    if run:
+                        flush()
+                else:
+                    mul_a(m, c)
+                    flush()
+                    mul_b(m, c)
+                    add(m, c, nc.gpsimd)
+        flush()

@@ -19,8 +19,8 @@ P = 128
 PASSES = W // 512
 FLOPS = 2 * B * N * W * H * A
 
-V_ADDS = (1, 4)
-V_ADDS_LAST = (1, 3, 5, 7)
+V_ADDS = ()
+V_ADDS_LAST = (5, 7)
 
 
 def tile_mha_pa_kernel(tc, x, w, out):
@@ -253,16 +253,12 @@ def tile_mha_pa_kernel(tc, x, w, out):
                 product(m, c)
                 run = False
                 if c == 0 and m == 1:
-                    sort_x(4)
-                    sort_x(5)
                     turn_x(4)
                     turn_x(5)
                     late_quants.extend([("x", 4, 0), ("x", 5, 0)])
                     run = True
                 if c == 0 and m == 3:
                     sort_w(1, 0, nc.vector.tensor_copy)
-                    sort_x(6)
-                    sort_x(7)
                     turn_x(6)
                     turn_x(7)
                     late_quants.extend([("x", 6, 0), ("x", 7, 0)])
@@ -274,14 +270,12 @@ def tile_mha_pa_kernel(tc, x, w, out):
                     turn_w(1, m - 4)
                     late_quants.append(("w", 1, m - 4))
                     run = True
-                if 0 < c < 3 and m == 2:
-                    sort_w(c + 1, 1, nc.scalar.copy)
-                if 0 < c < 3 and m in (1, 5):
+                if 0 < c < 3 and m in (0, 3):
+                    sort_w(c + 1, m // 3, nc.scalar.copy)
+                if 0 < c < 3 and m in (2, 5):
                     turn_w(c + 1, m // 4)
                     late_quants.append(("w", c + 1, m // 4))
                     run = True
-                if c < 2 and m == 6:
-                    sort_w(c + 2, 0, nc.scalar.copy)
                 if m in (V_ADDS_LAST if c == 3 else V_ADDS):
                     mul_a(m, c)
                     mul_b(m, c)

@@ -19,9 +19,6 @@ P = 128
 PASSES = W // 512
 FLOPS = 2 * B * N * W * H * A
 
-V_ADDS = ()
-V_ADDS_LAST = (5, 7)
-
 
 def tile_mha_pa_kernel(tc, x, w, out):
     nc = tc.nc
@@ -46,13 +43,9 @@ def tile_mha_pa_kernel(tc, x, w, out):
             x_raw.append(keep.tile([P, W], BF16, name="xraw%d" % m))
             nc.sync.dma_start(out=x_raw[m][:], in_=x_v[m // 2][m % 2])
         w_raw = {}
-
-        def load_w(q):
-            w_raw[q] = stage.tile([P, 2, W], BF16, name="wraw", bufs=4)
+        for q in range(2, 8):
+            w_raw[q] = keep.tile([P, 2, W], BF16, name="wraw%d" % q)
             nc.sync.dma_start(out=w_raw[q][:], in_=w_v2[q])
-
-        for q in range(2, 6):
-            load_w(q)
 
         warm = keep.tile([P, 1], F32, name="warm")
         nc.vector.memset(warm[:], 0.0)
@@ -119,8 +112,6 @@ def tile_mha_pa_kernel(tc, x, w, out):
         for m in range(2 * B):
             x_codes.append(keep.tile([P, PASSES * P], U32, name="xc%d" % m, align_bytes=64))
             x_scales.append(keep.tile([P, PASSES * P], U8, name="xs%d" % m, align_bytes=64))
-        x_sorted = {}
-        x_group = {}
         w_sorted = {}
         w_group = {}
         w_codes = {}
@@ -135,156 +126,106 @@ def tile_mha_pa_kernel(tc, x, w, out):
         def every_second(words):
             return [words[:, 256 * gg + u:256 * (gg + 1):2] for gg in range(2) for u in range(2)]
 
-        def sort_words(copy, dst, words):
-            copy(out=dst.rearrange("p (a u) j -> p a u j", u=2),
-                 in_=words.rearrange("p (a j u) -> p a u j", a=2, u=2))
-
-        def sort_w(c, gp, copy):
+        def sort_w(c, gp):
             w_sorted[(c, gp)] = stage.tile([P, 4, 4, P], F32, name="wsort", bufs=2)
             for hh in range(4):
-                sort_words(copy, w_sorted[(c, gp)][:, hh, :, :],
-                           w_raw[2 * c + hh // 2][:, hh % 2, 1024 * gp:1024 * (gp + 1)].bitcast(F32))
+                words = w_raw[2 * c + hh // 2][:, hh % 2, 1024 * gp:1024 * (gp + 1)].bitcast(F32)
+                nc.scalar.copy(out=w_sorted[(c, gp)][:, hh, :, :].rearrange("p (a u) j -> p a u j", u=2),
+                               in_=words.rearrange("p (a j u) -> p a u j", a=2, u=2))
 
-        def sort_x(m):
-            x_sorted[m] = stage.tile([P, 2, 4, P], F32, name="xsort", bufs=2)
-            for gp in range(2):
-                sort_words(nc.scalar.copy, x_sorted[m][:, gp, :, :],
-                           x_raw[m][:, 1024 * gp:1024 * (gp + 1)].bitcast(F32))
-
-        def turn_w(c, gp):
+        def prep_w(c, gp):
             if gp == 0:
                 w_group[c] = stage.tile([P, PASSES, 2048], BF16, name="gw", bufs=2, align_bytes=64)
+                w_codes[c] = stage.tile([P, PASSES, 512], U32, name="wc", bufs=2, align_bytes=64)
+                w_scales[c] = stage.tile([P, PASSES, 512], U8, name="ws", bufs=2, align_bytes=64)
             gwords = w_group[c][:].bitcast(F32)
             for hh in range(4):
                 if c == 0:
                     srcs = every_second(w0_raw[(hh, gp)][:].bitcast(F32))
+                elif c == 1:
+                    srcs = every_second(w_raw[2 + hh // 2][:, hh % 2, 1024 * gp:1024 * (gp + 1)].bitcast(F32))
                 else:
                     srcs = [w_sorted[(c, gp)][:, hh, j, :] for j in range(4)]
                 turn(srcs, gwords[:, 2 * gp:2 * gp + 2, 256 * hh:256 * (hh + 1)].rearrange(
                     "p a (r u) -> p a r u", u=2))
-
-        def quant_w(c, gp):
-            if gp == 0:
-                w_codes[c] = stage.tile([P, PASSES, 512], U32, name="wc", bufs=2, align_bytes=64)
-                w_scales[c] = stage.tile([P, PASSES, 512], U8, name="ws", bufs=2, align_bytes=64)
             two = slice(2 * gp, 2 * gp + 2)
             nc.vector.quantize_mx(out=w_codes[c][:, two, :].rearrange("p a n -> p (a n)").bitcast(E4X4),
                                   scales=w_scales[c][:, two, :].rearrange("p a n -> p (a n)"),
                                   in_=w_group[c][:, two, :].rearrange("p a n -> p (a n)"))
 
-        def turn_x(m):
-            x_group[m] = stage.tile([P, PASSES, 512], BF16, name="gx", bufs=2, align_bytes=64)
-            gwords = x_group[m][:].bitcast(F32)
+        def prep_x(m):
+            gx = stage.tile([P, PASSES, 512], BF16, name="gx", bufs=2, align_bytes=64)
+            gwords = gx[:].bitcast(F32)
+            words = x_raw[m][:].bitcast(F32)
             for gp in range(2):
-                if m in x_sorted:
-                    srcs = [x_sorted[m][:, gp, j, :] for j in range(4)]
-                else:
-                    srcs = every_second(x_raw[m][:, 1024 * gp:1024 * (gp + 1)].bitcast(F32))
-                turn(srcs, gwords[:, 2 * gp:2 * gp + 2, :].rearrange("p a (r u) -> p a r u", u=2))
-
-        def quant_x(m):
+                turn(every_second(words[:, 512 * gp:512 * (gp + 1)]),
+                     gwords[:, 2 * gp:2 * gp + 2, :].rearrange("p a (r u) -> p a r u", u=2))
             nc.vector.quantize_mx(out=x_codes[m][:].bitcast(E5X4), scales=x_scales[m][:],
-                                  in_=x_group[m][:].rearrange("p a n -> p (a n)"))
-
-        sums = {}
-        part_a = {}
-        part_b = {}
-        results = {}
-        added = set()
+                                  in_=gx[:].rearrange("p a n -> p (a n)"))
 
         def product(m, c):
-            sums[(m, c)] = psum_a.tile([P, 512], F32, name="acc")
+            acc = psum_a.tile([P, 512], F32, name="acc")
             for g in range(PASSES):
                 cols = slice(P * g, P * (g + 1))
-                nc.tensor.matmul_mx(out=sums[(m, c)][:], lhsT=x_codes[m][:, cols].bitcast(E5X4),
+                nc.tensor.matmul_mx(out=acc[:], lhsT=x_codes[m][:, cols].bitcast(E5X4),
                                     lhsT_scale=x_scales[m][:, cols],
                                     rhs=w_codes[c][:, g, :].bitcast(E4X4), rhs_scale=w_scales[c][:, g, :],
                                     start=(g == 0), stop=(g == PASSES - 1))
+            return acc
 
-        def mul_a(m, c):
-            part_a[(m, c)] = stage.tile([P, 512], F32, name="ta")
-            nc.vector.tensor_tensor(out=part_a[(m, c)][:], in0=sums[(m, c)][:],
-                                    in1=cos_t[:, m % 2, :, :].rearrange("p h a -> p (h a)"), op=ALU.mult)
-
-        def mul_b(m, c):
-            part_b[(m, c)] = stage.tile([P, 512], F32, name="tb")
-            nc.vector.tensor_tensor(out=part_b[(m, c)][:].rearrange("p (f e) -> p f e", e=2),
-                                    in0=sums[(m, c)][:].rearrange("p (f e) -> p f e", e=2)[:, :, ::-1],
-                                    in1=sin_t[:, m % 2, :, :].rearrange("p h (f e) -> p (h f) e", e=2),
+        def rotate(acc, i, res, adder):
+            ta = stage.tile([P, 512], F32, name="ta")
+            tb = stage.tile([P, 512], F32, name="tb")
+            nc.vector.tensor_tensor(out=ta[:], in0=acc[:], in1=cos_t[:, i, :, :].rearrange("p h a -> p (h a)"),
                                     op=ALU.mult)
+            nc.vector.tensor_tensor(out=tb[:].rearrange("p (f e) -> p f e", e=2),
+                                    in0=acc[:].rearrange("p (f e) -> p f e", e=2)[:, :, ::-1],
+                                    in1=sin_t[:, i, :, :].rearrange("p h (f e) -> p (h f) e", e=2),
+                                    op=ALU.mult)
+            adder.tensor_tensor(out=res[:, :, i, :], in0=ta[:].rearrange("p (h a) -> p h a", h=4),
+                                in1=tb[:].rearrange("p (h a) -> p h a", h=4), op=ALU.add)
 
-        def add(m, c, engine):
+        results = {}
+
+        def head_tile(m, c):
             b, i = m // 2, m % 2
-            if (b, c) not in results:
-                results[(b, c)] = stage.tile([P, 4, 2, A], F32, name="res")
-            res = results[(b, c)]
-            engine.tensor_tensor(out=res[:, :, i, :], in0=part_a[(m, c)][:].rearrange("p (h a) -> p h a", h=4),
-                                 in1=part_b[(m, c)][:].rearrange("p (h a) -> p h a", h=4), op=ALU.add)
-            added.add((m, c))
-            if c == 3 and b == B - 1:
-                nc.sync.dma_start(out=o_v[b][:, 4 * c:4 * c + 4, i, :], in_=res[:, :, i, :])
-            elif (2 * b, c) in added and (2 * b + 1, c) in added:
-                nc.sync.dma_start(out=o_v[b][:, 4 * c:4 * c + 4, :, :], in_=res[:])
+            last = (c == 3 and b == B - 1)
+            if i == 0:
+                results[b] = stage.tile([P, 4, 2, A], F32, name="res")
+            acc = product(m, c)
+            rotate(acc, i, results[b], nc.vector if (c == 3 and m in (5, 7)) else nc.gpsimd)
+            if last:
+                nc.sync.dma_start(out=o_v[b][:, 4 * c:4 * c + 4, i, :], in_=results[b][:, :, i, :])
+            elif i == 1:
+                nc.sync.dma_start(out=o_v[b][:, 4 * c:4 * c + 4, :, :], in_=results[b][:])
 
-        late_adds = []
-        late_quants = []
-
-        def flush():
-            for (m, c) in late_adds:
-                add(m, c, nc.vector)
-            late_adds.clear()
-            for (kind, p0, p1) in late_quants:
-                if kind == "x":
-                    quant_x(p0)
-                else:
-                    quant_w(p0, p1)
-            late_quants.clear()
-
-        turn_w(0, 0)
-        quant_w(0, 0)
+        prep_w(0, 0)
         finish_tables()
-        turn_w(0, 1)
-        quant_w(0, 1)
+        prep_w(0, 1)
         for m in range(4):
-            turn_x(m)
-            quant_x(m)
-        for c in range(4):
+            prep_x(m)
+        head_tile(0, 0)
+        head_tile(1, 0)
+        prep_x(4)
+        prep_x(5)
+        head_tile(2, 0)
+        head_tile(3, 0)
+        prep_x(6)
+        prep_x(7)
+        head_tile(4, 0)
+        prep_w(1, 0)
+        head_tile(5, 0)
+        prep_w(1, 1)
+        head_tile(6, 0)
+        head_tile(7, 0)
+        for c in range(1, 4):
             for m in range(8):
-                product(m, c)
-                run = False
-                if c == 0 and m == 1:
-                    turn_x(4)
-                    turn_x(5)
-                    late_quants.extend([("x", 4, 0), ("x", 5, 0)])
-                    run = True
-                if c == 0 and m == 3:
-                    sort_w(1, 0, nc.vector.tensor_copy)
-                    turn_x(6)
-                    turn_x(7)
-                    late_quants.extend([("x", 6, 0), ("x", 7, 0)])
-                    sort_w(1, 1, nc.vector.tensor_copy)
-                    load_w(6)
-                    load_w(7)
-                    run = True
-                if c == 0 and m in (4, 5):
-                    turn_w(1, m - 4)
-                    late_quants.append(("w", 1, m - 4))
-                    run = True
-                if 0 < c < 3 and m in (0, 3):
-                    sort_w(c + 1, m // 3, nc.scalar.copy)
-                if 0 < c < 3 and m in (2, 5):
-                    turn_w(c + 1, m // 4)
-                    late_quants.append(("w", c + 1, m // 4))
-                    run = True
-                if m in (V_ADDS_LAST if c == 3 else V_ADDS):
-                    mul_a(m, c)
-                    mul_b(m, c)
-                    late_adds.append((m, c))
-                    if run:
-                        flush()
-                else:
-                    mul_a(m, c)
-                    flush()
-                    mul_b(m, c)
-                    add(m, c, nc.gpsimd)
-        flush()
+                head_tile(m, c)
+                if c < 3 and m == 0:
+                    sort_w(c + 1, 0)
+                if c < 3 and m == 2:
+                    prep_w(c + 1, 0)
+                if c < 3 and m == 3:
+                    sort_w(c + 1, 1)
+                if c < 3 and m == 5:
+                    prep_w(c + 1, 1)

@@ -43,9 +43,13 @@ def tile_mha_pa_kernel(tc, x, w, out):
             x_raw.append(keep.tile([P, W], BF16, name="xraw%d" % m))
             nc.sync.dma_start(out=x_raw[m][:], in_=x_v[m // 2][m % 2])
         w_raw = {}
-        for q in range(2, 8):
+
+        def load_w(q):
             w_raw[q] = keep.tile([P, 2, W], BF16, name="wraw%d" % q)
             nc.sync.dma_start(out=w_raw[q][:], in_=w_v2[q])
+
+        load_w(2)
+        load_w(3)
 
         warm = keep.tile([P, 1], F32, name="warm")
         nc.vector.memset(warm[:], 0.0)
@@ -206,6 +210,8 @@ def tile_mha_pa_kernel(tc, x, w, out):
             prep_x(m)
         head_tile(0, 0)
         head_tile(1, 0)
+        load_w(4)
+        load_w(5)
         prep_x(4)
         prep_x(5)
         head_tile(2, 0)
@@ -218,6 +224,8 @@ def tile_mha_pa_kernel(tc, x, w, out):
         prep_w(1, 1)
         head_tile(6, 0)
         head_tile(7, 0)
+        load_w(6)
+        load_w(7)
         for c in range(1, 4):
             for m in range(8):
                 head_tile(m, c)

@@ -117,7 +117,6 @@ def tile_mha_pa_kernel(tc, x, w, out):
             x_codes.append(keep.tile([P, PASSES * P], U32, name="xc%d" % m, align_bytes=64))
             x_scales.append(keep.tile([P, PASSES * P], U8, name="xs%d" % m, align_bytes=64))
         w_sorted = {}
-        w_group = {}
         w_codes = {}
         w_scales = {}
 
@@ -138,11 +137,11 @@ def tile_mha_pa_kernel(tc, x, w, out):
                                in_=words.rearrange("p (a j u) -> p a u j", a=2, u=2))
 
         def prep_w(c, gp):
+            gw = stage.tile([P, 2, 2048], BF16, name="gw", bufs=2, align_bytes=64)
             if gp == 0:
-                w_group[c] = stage.tile([P, PASSES, 2048], BF16, name="gw", bufs=2, align_bytes=64)
                 w_codes[c] = stage.tile([P, PASSES, 512], U32, name="wc", bufs=2, align_bytes=64)
                 w_scales[c] = stage.tile([P, PASSES, 512], U8, name="ws", bufs=2, align_bytes=64)
-            gwords = w_group[c][:].bitcast(F32)
+            gwords = gw[:].bitcast(F32)
             for hh in range(4):
                 if c == 0:
                     srcs = every_second(w0_raw[(hh, gp)][:].bitcast(F32))
@@ -150,12 +149,11 @@ def tile_mha_pa_kernel(tc, x, w, out):
                     srcs = every_second(w_raw[2 + hh // 2][:, hh % 2, 1024 * gp:1024 * (gp + 1)].bitcast(F32))
                 else:
                     srcs = [w_sorted[(c, gp)][:, hh, j, :] for j in range(4)]
-                turn(srcs, gwords[:, 2 * gp:2 * gp + 2, 256 * hh:256 * (hh + 1)].rearrange(
-                    "p a (r u) -> p a r u", u=2))
+                turn(srcs, gwords[:, :, 256 * hh:256 * (hh + 1)].rearrange("p a (r u) -> p a r u", u=2))
             two = slice(2 * gp, 2 * gp + 2)
             nc.vector.quantize_mx(out=w_codes[c][:, two, :].rearrange("p a n -> p (a n)").bitcast(E4X4),
                                   scales=w_scales[c][:, two, :].rearrange("p a n -> p (a n)"),
-                                  in_=w_group[c][:, two, :].rearrange("p a n -> p (a n)"))
+                                  in_=gw[:].rearrange("p a n -> p (a n)"))
 
         def prep_x(m):
             gx = stage.tile([P, PASSES, 512], BF16, name="gx", bufs=2, align_bytes=64)
@@ -178,8 +176,8 @@ def tile_mha_pa_kernel(tc, x, w, out):
             return acc
 
         def rotate(acc, i, res, adder):
-            ta = stage.tile([P, 512], F32, name="ta")
-            tb = stage.tile([P, 512], F32, name="tb")
+            ta = stage.tile([P, 512], F32, name="ta", bufs=5)
+            tb = stage.tile([P, 512], F32, name="tb", bufs=5)
             nc.vector.tensor_tensor(out=ta[:], in0=acc[:], in1=cos_t[:, i, :, :].rearrange("p h a -> p (h a)"),
                                     op=ALU.mult)
             nc.vector.tensor_tensor(out=tb[:].rearrange("p (f e) -> p f e", e=2),
@@ -195,7 +193,7 @@ def tile_mha_pa_kernel(tc, x, w, out):
             b, i = m // 2, m % 2
             last = (c == 3 and b == B - 1)
             if i == 0:
-                results[b] = stage.tile([P, 4, 2, A], F32, name="res")
+                results[b] = stage.tile([P, 4, 2, A], F32, name="res", bufs=4)
             acc = product(m, c)
             rotate(acc, i, results[b], nc.vector if (c == 3 and m in (5, 7)) else nc.gpsimd)
             if last:
@@ -223,17 +221,18 @@ def tile_mha_pa_kernel(tc, x, w, out):
         head_tile(5, 0)
         prep_w(1, 1)
         head_tile(6, 0)
+        sort_w(2, 0)
         head_tile(7, 0)
         load_w(6)
         load_w(7)
         for c in range(1, 4):
             for m in range(8):
                 head_tile(m, c)
-                if c < 3 and m == 0:
-                    sort_w(c + 1, 0)
-                if c < 3 and m == 2:
+                if c < 3 and m == 1:
                     prep_w(c + 1, 0)
-                if c < 3 and m == 3:
+                if c < 3 and m == 2:
                     sort_w(c + 1, 1)
-                if c < 3 and m == 5:
+                if c < 3 and m == 4:
                     prep_w(c + 1, 1)
+                if c < 2 and m == 6:
+                    sort_w(c + 2, 0)

@@ -104,9 +104,9 @@ def tile_mha_pa_kernel(tc, x, w, out):
             nc.scalar.activation(out=sc[:].rearrange("p i s f -> p (i s f)"), in_=ang_f, func=ACT.Sin)
             nc.vector.tensor_copy(out=cos1[:, :, :, 0], in_=sc[:, :, 1, :])
             nc.vector.tensor_copy(out=cos1[:, :, :, 1], in_=sc[:, :, 1, :])
-            nc.vector.tensor_scalar(out=sin1[:, :, :, 0], in0=sc[:, :, 0, :], scalar1=-1.0, scalar2=None,
+            nc.vector.tensor_scalar(out=sin1[:, :, :, 1], in0=sc[:, :, 0, :], scalar1=-1.0, scalar2=None,
                                     op0=ALU.mult)
-            nc.vector.tensor_copy(out=sin1[:, :, :, 1], in_=sc[:, :, 0, :])
+            nc.vector.tensor_copy(out=sin1[:, :, :, 0], in_=sc[:, :, 0, :])
             for hh in range(4):
                 nc.vector.tensor_copy(out=cos_t[:, :, hh, :], in_=cos1[:].rearrange("p i f e -> p i (f e)"))
                 nc.vector.tensor_copy(out=sin_t[:, :, hh, :], in_=sin1[:].rearrange("p i f e -> p i (f e)"))
@@ -180,12 +180,11 @@ def tile_mha_pa_kernel(tc, x, w, out):
             tb = stage.tile([P, 512], F32, name="tb", bufs=5)
             nc.vector.tensor_tensor(out=ta[:], in0=acc[:], in1=cos_t[:, i, :, :].rearrange("p h a -> p (h a)"),
                                     op=ALU.mult)
-            nc.vector.tensor_tensor(out=tb[:].rearrange("p (f e) -> p f e", e=2),
-                                    in0=acc[:].rearrange("p (f e) -> p f e", e=2)[:, :, ::-1],
-                                    in1=sin_t[:, i, :, :].rearrange("p h (f e) -> p (h f) e", e=2),
+            nc.vector.tensor_tensor(out=tb[:], in0=acc[:], in1=sin_t[:, i, :, :].rearrange("p h a -> p (h a)"),
                                     op=ALU.mult)
-            adder.tensor_tensor(out=res[:, :, i, :], in0=ta[:].rearrange("p (h a) -> p h a", h=4),
-                                in1=tb[:].rearrange("p (h a) -> p h a", h=4), op=ALU.add)
+            adder.tensor_tensor(out=res[:, :, i, :].rearrange("p h (f e) -> p h f e", e=2),
+                                in0=ta[:].rearrange("p (h f e) -> p h f e", h=4, e=2),
+                                in1=tb[:].rearrange("p (h f e) -> p h f e", h=4, e=2)[:, :, :, ::-1], op=ALU.add)
 
         results = {}
 

@@ -97,8 +97,7 @@ def tile_mha_pa_kernel(tc, x, w, out):
         sc = keep.tile([P, 2, 2, 64], F32, name="sc")
         cos1 = keep.tile([P, 2, 64, 2], F32, name="cos1")
         sin1 = keep.tile([P, 2, 64, 2], F32, name="sin1")
-        cos_t = keep.tile([P, 2, 4, A], F32, name="cos_t")
-        sin_t = keep.tile([P, 2, 4, A], F32, name="sin_t")
+        factors = keep.tile([P, 2, 2, 4, A], F32, name="factors")
 
         def finish_tables():
             nc.scalar.activation(out=sc[:].rearrange("p i s f -> p (i s f)"), in_=ang_f, func=ACT.Sin)
@@ -108,8 +107,8 @@ def tile_mha_pa_kernel(tc, x, w, out):
                                     op0=ALU.mult)
             nc.vector.tensor_copy(out=sin1[:, :, :, 0], in_=sc[:, :, 0, :])
             for hh in range(4):
-                nc.vector.tensor_copy(out=cos_t[:, :, hh, :], in_=cos1[:].rearrange("p i f e -> p i (f e)"))
-                nc.vector.tensor_copy(out=sin_t[:, :, hh, :], in_=sin1[:].rearrange("p i f e -> p i (f e)"))
+                nc.vector.tensor_copy(out=factors[:, :, 0, hh, :], in_=cos1[:].rearrange("p i f e -> p i (f e)"))
+                nc.vector.tensor_copy(out=factors[:, :, 1, hh, :], in_=sin1[:].rearrange("p i f e -> p i (f e)"))
 
         x_codes = []
         x_scales = []
@@ -176,15 +175,13 @@ def tile_mha_pa_kernel(tc, x, w, out):
             return acc
 
         def rotate(acc, i, res, adder):
-            ta = stage.tile([P, 512], F32, name="ta", bufs=5)
-            tb = stage.tile([P, 512], F32, name="tb", bufs=5)
-            nc.vector.tensor_tensor(out=ta[:], in0=acc[:], in1=cos_t[:, i, :, :].rearrange("p h a -> p (h a)"),
-                                    op=ALU.mult)
-            nc.vector.tensor_tensor(out=tb[:], in0=acc[:], in1=sin_t[:, i, :, :].rearrange("p h a -> p (h a)"),
-                                    op=ALU.mult)
+            prod = stage.tile([P, 2, 512], F32, name="prod", bufs=5)
+            nc.vector.tensor_tensor(out=prod[:], in0=acc[:].unsqueeze(1).to_broadcast([P, 2, 512]),
+                                    in1=factors[:, i, :, :, :].rearrange("p s h a -> p s (h a)"), op=ALU.mult)
             adder.tensor_tensor(out=res[:, :, i, :].rearrange("p h (f e) -> p h f e", e=2),
-                                in0=ta[:].rearrange("p (h f e) -> p h f e", h=4, e=2),
-                                in1=tb[:].rearrange("p (h f e) -> p h f e", h=4, e=2)[:, :, :, ::-1], op=ALU.add)
+                                in0=prod[:, 0, :].rearrange("p (h f e) -> p h f e", h=4, e=2),
+                                in1=prod[:, 1, :].rearrange("p (h f e) -> p h f e", h=4, e=2)[:, :, :, ::-1],
+                                op=ALU.add)
 
         results = {}
 

@@ -141,18 +141,28 @@ def tile_mha_pa_kernel(tc, x, w, out):
                 w_codes[c] = stage.tile([P, PASSES, 512], U32, name="wc", bufs=2, align_bytes=64)
                 w_scales[c] = stage.tile([P, PASSES, 512], U8, name="ws", bufs=2, align_bytes=64)
             gwords = gw[:].bitcast(F32)
+            views = []
             for hh in range(4):
                 if c == 0:
-                    srcs = every_second(w0_raw[(hh, gp)][:].bitcast(F32))
+                    views.append(every_second(w0_raw[(hh, gp)][:].bitcast(F32)))
                 elif c == 1:
-                    srcs = every_second(w_raw[2 + hh // 2][:, hh % 2, 1024 * gp:1024 * (gp + 1)].bitcast(F32))
+                    views.append(every_second(w_raw[2 + hh // 2][:, hh % 2, 1024 * gp:1024 * (gp + 1)].bitcast(F32)))
                 else:
-                    srcs = [w_sorted[(c, gp)][:, hh, j, :] for j in range(4)]
-                turn(srcs, gwords[:, :, 256 * hh:256 * (hh + 1)].rearrange("p a (r u) -> p a r u", u=2))
-            two = slice(2 * gp, 2 * gp + 2)
-            nc.vector.quantize_mx(out=w_codes[c][:, two, :].rearrange("p a n -> p (a n)").bitcast(E4X4),
-                                  scales=w_scales[c][:, two, :].rearrange("p a n -> p (a n)"),
-                                  in_=gw[:].rearrange("p a n -> p (a n)"))
+                    views.append([w_sorted[(c, gp)][:, hh, j, :] for j in range(4)])
+            if c == 0:
+                for hh in range(4):
+                    turn(views[hh], gwords[:, :, 256 * hh:256 * (hh + 1)].rearrange("p a (r u) -> p a r u", u=2))
+                two = slice(2 * gp, 2 * gp + 2)
+                nc.vector.quantize_mx(out=w_codes[c][:, two, :].rearrange("p a n -> p (a n)").bitcast(E4X4),
+                                      scales=w_scales[c][:, two, :].rearrange("p a n -> p (a n)"),
+                                      in_=gw[:].rearrange("p a n -> p (a n)"))
+                return
+            for a in range(2):
+                for hp in range(2):
+                    srcs = [views[2 * hp + h][2 * a + u] for h in range(2) for u in range(2)]
+                    turn(srcs, gwords[:, a, 512 * hp:512 * (hp + 1)].rearrange("p (h r u) -> p h r u", h=2, u=2))
+                nc.vector.quantize_mx(out=w_codes[c][:, 2 * gp + a, :].bitcast(E4X4),
+                                      scales=w_scales[c][:, 2 * gp + a, :], in_=gw[:, a, :])
 
         def prep_x(m):
             gx = stage.tile([P, PASSES, 512], BF16, name="gx", bufs=2, align_bytes=64)

@@ -161,8 +161,10 @@ def tile_mha_pa_kernel(tc, x, w, out):
                 for hp in range(2):
                     srcs = [views[2 * hp + h][2 * a + u] for h in range(2) for u in range(2)]
                     turn(srcs, gwords[:, a, 512 * hp:512 * (hp + 1)].rearrange("p (h r u) -> p h r u", h=2, u=2))
-                nc.vector.quantize_mx(out=w_codes[c][:, 2 * gp + a, :].bitcast(E4X4),
-                                      scales=w_scales[c][:, 2 * gp + a, :], in_=gw[:, a, :])
+                    cols = slice(256 * hp, 256 * (hp + 1))
+                    nc.vector.quantize_mx(out=w_codes[c][:, 2 * gp + a, cols].bitcast(E4X4),
+                                          scales=w_scales[c][:, 2 * gp + a, cols],
+                                          in_=gw[:, a, 1024 * hp:1024 * (hp + 1)])
 
         def prep_x(m):
             gx = stage.tile([P, PASSES, 512], BF16, name="gx", bufs=2, align_bytes=64)
@@ -171,8 +173,9 @@ def tile_mha_pa_kernel(tc, x, w, out):
             for gp in range(2):
                 turn(every_second(words[:, 512 * gp:512 * (gp + 1)]),
                      gwords[:, 2 * gp:2 * gp + 2, :].rearrange("p a (r u) -> p a r u", u=2))
-            nc.vector.quantize_mx(out=x_codes[m][:].bitcast(E5X4), scales=x_scales[m][:],
-                                  in_=gx[:].rearrange("p a n -> p (a n)"))
+                cols = slice(256 * gp, 256 * (gp + 1))
+                nc.vector.quantize_mx(out=x_codes[m][:, cols].bitcast(E5X4), scales=x_scales[m][:, cols],
+                                      in_=gx[:, 2 * gp:2 * gp + 2, :].rearrange("p a n -> p (a n)"))
 
         def product(m, c):
             acc = psum_a.tile([P, 512], F32, name="acc")

@@ -198,17 +198,38 @@ def tile_mha_pa_kernel(tc, x, w, out):
 
         results = {}
 
+        late = {}
+
         def head_tile(m, c):
             b, i = m // 2, m % 2
-            last = (c == 3 and b == B - 1)
+            last = (c == 3 and b in (1, B - 1))
             if i == 0:
                 results[b] = stage.tile([P, 4, 2, A], F32, name="res", bufs=4)
             acc = product(m, c)
-            rotate(acc, i, results[b], nc.vector if (c == 3 and m in (5, 7)) else nc.gpsimd)
+            if c == 3 and m == 7:
+                late_add()
+            if c == 3 and m == 3:
+                prod = stage.tile([P, 2, 512], F32, name="prod", bufs=5)
+                nc.vector.tensor_tensor(out=prod[:, 0, :], in0=acc[:],
+                                        in1=factors[:, i, 0, :, :].rearrange("p h a -> p (h a)"), op=ALU.mult)
+                nc.vector.tensor_tensor(out=prod[:, 1, :].rearrange("p (f e) -> p f e", e=2),
+                                        in0=acc[:].rearrange("p (f e) -> p f e", e=2)[:, :, ::-1],
+                                        in1=factors[:, i, 1, :, :].rearrange("p h (f e) -> p (h f) e", e=2)[:, :, ::-1],
+                                        op=ALU.mult)
+                late[0] = prod
+                return
+            rotate(acc, i, results[b], nc.vector if (c == 3 and m == 7) else nc.gpsimd)
             if last:
                 nc.sync.dma_start(out=o_v[b][:, 4 * c:4 * c + 4, i, :], in_=results[b][:, :, i, :])
             elif i == 1:
                 nc.sync.dma_start(out=o_v[b][:, 4 * c:4 * c + 4, :, :], in_=results[b][:])
+
+        def late_add():
+            total = psum_t.tile([P, 512], F32, name="tp")
+            nc.tensor.matmul(out=total[:], lhsT=ident[:], rhs=late[0][:, 0, :], start=True, stop=False)
+            nc.tensor.matmul(out=total[:], lhsT=ident[:], rhs=late[0][:, 1, :], start=False, stop=True)
+            nc.scalar.copy(out=results[1][:, :, 1, :], in_=total[:].rearrange("p (h a) -> p h a", h=4))
+            nc.sync.dma_start(out=o_v[1][:, 12:16, 1, :], in_=results[1][:, :, 1, :])
 
         prep_w(0, 0)
         finish_tables()

@@ -225,11 +225,14 @@ def tile_mha_pa_kernel(tc, x, w, out):
                 nc.sync.dma_start(out=o_v[b][:, 4 * c:4 * c + 4, :, :], in_=results[b][:])
 
         def late_add():
-            total = psum_t.tile([P, 512], F32, name="tp")
-            nc.tensor.matmul(out=total[:], lhsT=ident[:], rhs=late[0][:, 0, :], start=True, stop=False)
-            nc.tensor.matmul(out=total[:], lhsT=ident[:], rhs=late[0][:, 1, :], start=False, stop=True)
-            nc.scalar.copy(out=results[1][:, :, 1, :], in_=total[:].rearrange("p (h a) -> p h a", h=4))
-            nc.sync.dma_start(out=o_v[1][:, 12:16, 1, :], in_=results[1][:, :, 1, :])
+            for half in range(2):
+                cols = slice(256 * half, 256 * (half + 1))
+                heads = slice(2 * half, 2 * half + 2)
+                total = psum_t.tile([P, 256], F32, name="tp")
+                nc.tensor.matmul(out=total[:], lhsT=ident[:], rhs=late[0][:, 0, cols], start=True, stop=False)
+                nc.tensor.matmul(out=total[:], lhsT=ident[:], rhs=late[0][:, 1, cols], start=False, stop=True)
+                nc.scalar.copy(out=results[1][:, heads, 1, :], in_=total[:].rearrange("p (h a) -> p h a", h=2))
+                nc.scalar.dma_start(out=o_v[1][:, 12 + 2 * half:14 + 2 * half, 1, :], in_=results[1][:, heads, 1, :])
 
         prep_w(0, 0)
         finish_tables()
@@ -258,11 +261,11 @@ def tile_mha_pa_kernel(tc, x, w, out):
         for c in range(1, 4):
             for m in range(8):
                 head_tile(m, c)
-                if c < 3 and m == 1:
-                    prep_w(c + 1, 0)
                 if c < 3 and m == 2:
+                    prep_w(c + 1, 0)
+                if c < 3 and m == 3:
                     sort_w(c + 1, 1)
-                if c < 3 and m == 4:
+                if c < 3 and m == 5:
                     prep_w(c + 1, 1)
                 if c < 2 and m == 6:
                     sort_w(c + 2, 0)

import math
from contextlib import ExitStack

import concourse.mybir as mybir
from concourse.masks import make_identity

F32 = mybir.dt.float32
BF16 = mybir.dt.bfloat16
U32 = mybir.dt.uint32
U8 = mybir.dt.uint8
I32 = mybir.dt.int32
E5X4 = mybir.dt.float8_e5m2_x4
E4X4 = mybir.dt.float8_e4m3fn_x4
ALU = mybir.AluOpType
ACT = mybir.ActivationFunctionType

B, N, W, H, A = 4, 256, 2048, 16, 128
P = 128
PASSES = W // 512
FLOPS = 2 * B * N * W * H * A


def tile_mha_pa_kernel(tc, x, w, out):
    nc = tc.nc
    with ExitStack() as ctx:
        ctx.enter_context(tc.manual_schedule())
        keep = ctx.enter_context(tc.tile_pool(name="keep", bufs=1))
        stage = ctx.enter_context(tc.tile_pool(name="stage", bufs=3))
        psum_t = ctx.enter_context(tc.psum_pool(name="psum_t", bufs=4))
        psum_a = ctx.enter_context(tc.psum_pool(name="psum_a", bufs=4))

        x_v = x.rearrange("b (p i) k -> b i p k", i=2)
        w_v = w.rearrange("(h p) k -> h p k", p=P)
        w_v2 = w.rearrange("(q e p) k -> q p e k", p=P, e=2)
        o_v = out.rearrange("b h (p i) a -> b p h i a", i=2)
        w0_raw = {}
        for gp in range(2):
            for hh in range(4):
                w0_raw[(hh, gp)] = keep.tile([P, 1024], BF16, name="w0raw%d_%d" % (hh, gp))
                nc.sync.dma_start(out=w0_raw[(hh, gp)][:], in_=w_v[hh][:, 1024 * gp:1024 * (gp + 1)])
        x_raw = []
        for m in range(2 * B):
            x_raw.append(keep.tile([P, W], BF16, name="xraw%d" % m))
            nc.sync.dma_start(out=x_raw[m][:], in_=x_v[m // 2][m % 2])
        w_raw = {}

        def load_w(q):
            w_raw[q] = keep.tile([P, 2, W], BF16, name="wraw%d" % q)
            nc.sync.dma_start(out=w_raw[q][:], in_=w_v2[q])

        load_w(2)
        load_w(3)

        warm = keep.tile([P, 1], F32, name="warm")
        nc.vector.memset(warm[:], 0.0)
        nc.scalar.activation(out=warm[:], in_=warm[:], func=ACT.Sin)

        ident = keep.tile([P, P], F32, name="ident")
        make_identity(nc, ident[:])

        pos = keep.tile([P, 2], F32, name="pos")
        nc.gpsimd.iota(pos[:], pattern=[[1, 2]], base=0, channel_multiplier=2,
                       allow_small_or_imprecise_dtypes=True)
        ones = keep.tile([P, 8], F32, name="ones")
        nc.vector.memset(ones[:], 1.0)
        frq = keep.tile([P, 8, 8], F32, name="frq")
        for a in range(8):
            nc.vector.tensor_scalar(out=frq[:, a, :], in0=ones[:], scalar1=10000.0 ** (-8.0 * a / 63.0),
                                    scalar2=None, op0=ALU.mult)
        for c in range(1, 8):
            nc.vector.tensor_scalar(out=frq[:, :, c], in0=frq[:, :, c], scalar1=10000.0 ** (-1.0 * c / 63.0),
                                    scalar2=None, op0=ALU.mult)
        ang = keep.tile([P, 2, 2, 64], F32, name="ang")
        for i in range(2):
            for s in range(2):
                nc.vector.tensor_scalar(out=ang[:, i, s, :], in0=frq[:].rearrange("p a c -> p (a c)"),
                                        scalar1=pos[:, i:i + 1], scalar2=s * math.pi / 2.0,
                                        op0=ALU.mult, op1=ALU.add)
        ang_f = ang[:].rearrange("p i s f -> p (i s f)")
        turns_i = keep.tile([P, 256], I32, name="turns_i")
        nc.vector.tensor_scalar(out=turns_i[:], in0=ang_f, scalar1=1.0 / (2.0 * math.pi), scalar2=None,
                                op0=ALU.mult)
        turns = keep.tile([P, 256], F32, name="turns")
        nc.vector.tensor_copy(out=turns[:], in_=turns_i[:])
        c_hi = 6.28125
        c_lo = 2.0 * math.pi - c_hi
        nc.vector.scalar_tensor_tensor(out=ang_f, in0=turns[:], scalar=-c_hi, in1=ang_f,
                                       op0=ALU.mult, op1=ALU.add)
        nc.vector.scalar_tensor_tensor(out=ang_f, in0=turns[:], scalar=-c_lo, in1=ang_f,
                                       op0=ALU.mult, op1=ALU.add)
        nc.vector.tensor_scalar(out=turns[:], in0=ang_f, scalar1=math.pi, scalar2=-2.0 * math.pi,
                                op0=ALU.is_gt, op1=ALU.mult)
        nc.vector.tensor_tensor(out=ang_f, in0=ang_f, in1=turns[:], op=ALU.add)
        nc.vector.tensor_scalar(out=turns[:], in0=ang_f, scalar1=-math.pi, scalar2=2.0 * math.pi,
                                op0=ALU.is_lt, op1=ALU.mult)
        nc.vector.tensor_tensor(out=ang_f, in0=ang_f, in1=turns[:], op=ALU.add)
        sc = keep.tile([P, 2, 2, 64], F32, name="sc")
        cos1 = keep.tile([P, 2, 64, 2], F32, name="cos1")
        sin1 = keep.tile([P, 2, 64, 2], F32, name="sin1")
        factors = keep.tile([P, 2, 2, 4, A], F32, name="factors")

        def finish_tables():
            nc.scalar.activation(out=sc[:].rearrange("p i s f -> p (i s f)"), in_=ang_f, func=ACT.Sin)
            nc.vector.tensor_copy(out=cos1[:, :, :, 0], in_=sc[:, :, 1, :])
            nc.vector.tensor_copy(out=cos1[:, :, :, 1], in_=sc[:, :, 1, :])
            nc.vector.tensor_scalar(out=sin1[:, :, :, 1], in0=sc[:, :, 0, :], scalar1=-1.0, scalar2=None,
                                    op0=ALU.mult)
            nc.vector.tensor_copy(out=sin1[:, :, :, 0], in_=sc[:, :, 0, :])
            for hh in range(4):
                nc.vector.tensor_copy(out=factors[:, :, 0, hh, :], in_=cos1[:].rearrange("p i f e -> p i (f e)"))
                nc.vector.tensor_copy(out=factors[:, :, 1, hh, :], in_=sin1[:].rearrange("p i f e -> p i (f e)"))

        x_codes = []
        x_scales = []
        for m in range(2 * B):
            x_codes.append(keep.tile([P, PASSES * P], U32, name="xc%d" % m, align_bytes=64))
            x_scales.append(keep.tile([P, PASSES * P], U8, name="xs%d" % m, align_bytes=64))
        w_sorted = {}
        w_codes = {}
        w_scales = {}

        def turn(srcs, dst):
            tp = psum_t.tile([P, 2, 2, P], F32, name="tp")
            for j in range(4):
                nc.tensor.transpose(out=tp[:, j // 2, j % 2, :], in_=srcs[j], identity=ident[:])
            nc.scalar.copy(out=dst, in_=tp[:].rearrange("p a u r -> p a r u"))

        def every_second(words):
            return [words[:, 256 * gg + u:256 * (gg + 1):2] for gg in range(2) for u in range(2)]

        def sort_w(c, gp):
            w_sorted[(c, gp)] = stage.tile([P, 4, 4, P], F32, name="wsort", bufs=2)
            for hh in range(4):
                words = w_raw[2 * c + hh // 2][:, hh % 2, 1024 * gp:1024 * (gp + 1)].bitcast(F32)
                nc.scalar.copy(out=w_sorted[(c, gp)][:, hh, :, :].rearrange("p (a u) j -> p a u j", u=2),
                               in_=words.rearrange("p (a j u) -> p a u j", a=2, u=2))

        def prep_w(c, gp):
            gw = stage.tile([P, 2, 2048], BF16, name="gw", bufs=2, align_bytes=64)
            if gp == 0:
                w_codes[c] = stage.tile([P, PASSES, 512], U32, name="wc", bufs=2, align_bytes=64)
                w_scales[c] = stage.tile([P, PASSES, 512], U8, name="ws", bufs=2, align_bytes=64)
            gwords = gw[:].bitcast(F32)
            views = []
            for hh in range(4):
                if c == 0:
                    views.append(every_second(w0_raw[(hh, gp)][:].bitcast(F32)))
                elif c == 1:
                    views.append(every_second(w_raw[2 + hh // 2][:, hh % 2, 1024 * gp:1024 * (gp + 1)].bitcast(F32)))
                else:
                    views.append([w_sorted[(c, gp)][:, hh, j, :] for j in range(4)])
            if c == 0:
                for hh in range(4):
                    turn(views[hh], gwords[:, :, 256 * hh:256 * (hh + 1)].rearrange("p a (r u) -> p a r u", u=2))
                two = slice(2 * gp, 2 * gp + 2)
                nc.vector.quantize_mx(out=w_codes[c][:, two, :].rearrange("p a n -> p (a n)").bitcast(E4X4),
                                      scales=w_scales[c][:, two, :].rearrange("p a n -> p (a n)"),
                                      in_=gw[:].rearrange("p a n -> p (a n)"))
                return
            for a in range(2):
                for hp in range(2):
                    srcs = [views[2 * hp + h][2 * a + u] for h in range(2) for u in range(2)]
                    turn(srcs, gwords[:, a, 512 * hp:512 * (hp + 1)].rearrange("p (h r u) -> p h r u", h=2, u=2))
                    cols = slice(256 * hp, 256 * (hp + 1))
                    nc.vector.quantize_mx(out=w_codes[c][:, 2 * gp + a, cols].bitcast(E4X4),
                                          scales=w_scales[c][:, 2 * gp + a, cols],
                                          in_=gw[:, a, 1024 * hp:1024 * (hp + 1)])

        def prep_x(m):
            gx = stage.tile([P, PASSES, 512], BF16, name="gx", bufs=2, align_bytes=64)
            gwords = gx[:].bitcast(F32)
            words = x_raw[m][:].bitcast(F32)
            for gp in range(2):
                turn(every_second(words[:, 512 * gp:512 * (gp + 1)]),
                     gwords[:, 2 * gp:2 * gp + 2, :].rearrange("p a (r u) -> p a r u", u=2))
                cols = slice(256 * gp, 256 * (gp + 1))
                nc.vector.quantize_mx(out=x_codes[m][:, cols].bitcast(E5X4), scales=x_scales[m][:, cols],
                                      in_=gx[:, 2 * gp:2 * gp + 2, :].rearrange("p a n -> p (a n)"))

        def product(m, c):
            acc = psum_a.tile([P, 512], F32, name="acc")
            for g in range(PASSES):
                cols = slice(P * g, P * (g + 1))
                nc.tensor.matmul_mx(out=acc[:], lhsT=x_codes[m][:, cols].bitcast(E5X4),
                                    lhsT_scale=x_scales[m][:, cols],
                                    rhs=w_codes[c][:, g, :].bitcast(E4X4), rhs_scale=w_scales[c][:, g, :],
                                    start=(g == 0), stop=(g == PASSES - 1))
            return acc

        def rotate(acc, i, res, adder):
            prod = stage.tile([P, 2, 512], F32, name="prod", bufs=5)
            nc.vector.tensor_tensor(out=prod[:], in0=acc[:].unsqueeze(1).to_broadcast([P, 2, 512]),
                                    in1=factors[:, i, :, :, :].rearrange("p s h a -> p s (h a)"), op=ALU.mult)
            adder.tensor_tensor(out=res[:, :, i, :].rearrange("p h (f e) -> p h f e", e=2),
                                in0=prod[:, 0, :].rearrange("p (h f e) -> p h f e", h=4, e=2),
                                in1=prod[:, 1, :].rearrange("p (h f e) -> p h f e", h=4, e=2)[:, :, :, ::-1],
                                op=ALU.add)

        results = {}

        late = {}

        def head_tile(m, c):
            b, i = m // 2, m % 2
            last = (c == 3 and b in (1, B - 1))
            if i == 0:
                results[b] = stage.tile([P, 4, 2, A], F32, name="res", bufs=4)
            acc = product(m, c)
            if c == 3 and m == 7:
                late_add()
            if c == 3 and m == 3:
                prod = stage.tile([P, 2, 512], F32, name="prod", bufs=5)
                nc.vector.tensor_tensor(out=prod[:, 0, :], in0=acc[:],
                                        in1=factors[:, i, 0, :, :].rearrange("p h a -> p (h a)"), op=ALU.mult)
                nc.vector.tensor_tensor(out=prod[:, 1, :].rearrange("p (f e) -> p f e", e=2),
                                        in0=acc[:].rearrange("p (f e) -> p f e", e=2)[:, :, ::-1],
                                        in1=factors[:, i, 1, :, :].rearrange("p h (f e) -> p (h f) e", e=2)[:, :, ::-1],
                                        op=ALU.mult)
                late[0] = prod
                return
            rotate(acc, i, results[b], nc.vector if (c == 3 and m == 7) else nc.gpsimd)
            if last:
                nc.sync.dma_start(out=o_v[b][:, 4 * c:4 * c + 4, i, :], in_=results[b][:, :, i, :])
            elif i == 1:
                nc.sync.dma_start(out=o_v[b][:, 4 * c:4 * c + 4, :, :], in_=results[b][:])

        def late_add():
            for half in range(2):
                cols = slice(256 * half, 256 * (half + 1))
                heads = slice(2 * half, 2 * half + 2)
                total = psum_t.tile([P, 256], F32, name="tp")
                nc.tensor.matmul(out=total[:], lhsT=ident[:], rhs=late[0][:, 0, cols], start=True, stop=False)
                nc.tensor.matmul(out=total[:], lhsT=ident[:], rhs=late[0][:, 1, cols], start=False, stop=True)
                nc.scalar.copy(out=results[1][:, heads, 1, :], in_=total[:].rearrange("p (h a) -> p h a", h=2))
                nc.scalar.dma_start(out=o_v[1][:, 12 + 2 * half:14 + 2 * half, 1, :], in_=results[1][:, heads, 1, :])

        prep_w(0, 0)
        finish_tables()
        prep_w(0, 1)
        for m in range(4):
            prep_x(m)
        head_tile(0, 0)
        head_tile(1, 0)
        load_w(4)
        load_w(5)
        prep_x(4)
        prep_x(5)
        head_tile(2, 0)
        head_tile(3, 0)
        prep_x(6)
        prep_x(7)
        head_tile(4, 0)
        prep_w(1, 0)
        head_tile(5, 0)
        prep_w(1, 1)
        head_tile(6, 0)
        sort_w(2, 0)
        head_tile(7, 0)
        load_w(6)
        load_w(7)
        for c in range(1, 4):
            for m in range(8):
                head_tile(m, c)
                if c < 3 and m == 2:
                    prep_w(c + 1, 0)
                if c < 3 and m == 3:
                    sort_w(c + 1, 1)
                if c < 3 and m == 5:
                    prep_w(c + 1, 1)
                if c < 2 and m == 6:
                    sort_w(c + 2, 0)
